import numpy as np
import ml_dtypes


def mxq(x, axis, fmt="e4m3"):
    dtype, down = {"e4m3": (ml_dtypes.float8_e4m3fn, 7), "e5m2": (ml_dtypes.float8_e5m2, 14)}[fmt]
    v = np.moveaxis(np.asarray(x, np.float32).astype(ml_dtypes.bfloat16).astype(np.float64), axis, -1)
    blocks = v.reshape(v.shape[:-1] + (-1, 32))
    amax = np.abs(blocks).max(-1, keepdims=True)
    byte = np.maximum(np.where(amax > 0, np.frexp(amax)[1] - 1 + 127, 0) - down, 1)
    scale = np.exp2(byte - 127.0)
    codes = (blocks / scale).astype(np.float32).astype(dtype).astype(np.float64)
    return np.moveaxis((codes * scale).reshape(v.shape), -1, axis)


WIDE = False


def mx_kscale(k):
    if not WIDE:
        return np.ones(k)
    levels = np.array([10, -10, 5, -5, 0])
    a = np.random.permutation(np.resize(levels, k // 512 * 4)).reshape(k // 512, 4)
    idx = np.arange(k)
    return np.exp2(a[idx // 512, idx % 128 // 32])


BF16 = ml_dtypes.bfloat16


def bf(x):
    return np.asarray(x, np.float32).astype(BF16)


def f64(x):
    return np.asarray(x).astype(np.float64)


B, C, H, W = 1, 512, 64, 32
CH = C // 2
N = H * W
QS = 1.35 * CH ** -0.25


def pool2(t):
    r = t.reshape(B, -1, H // 2, 2, W // 2, 2)
    return r.max(axis=(3, 5)) + r.mean(axis=(3, 5))


def setup_inputs():
    s = mx_kscale(C)
    return {"x": bf(np.random.standard_normal((B, C, H, W)) * s[None, :, None, None]),
            "W1": bf(np.random.standard_normal((CH, C)) * QS / np.sqrt(C) / s),
            "W2": bf(np.random.standard_normal((CH, C)) * QS / np.sqrt(C) / s)}


def reference(x, W1, W2):
    xq = mxq(f64(x).reshape(B, C, N), 1, "e4m3")
    c1 = mxq(f64(W1), 1, "e4m3") @ xq
    c2 = mxq(f64(W2), 1, "e4m3") @ xq
    return pool2(c1.reshape(B, CH, H, W)), c2.reshape(B, CH, H, W)

@@ -1,0 +1,136 @@
+from contextlib import ExitStack
+
+import concourse.masks as masks
+import concourse.mybir as mybir
+
+FLOPS = 2 * 512 * 512 * 2048
+
+BF16 = mybir.dt.bfloat16
+F32 = mybir.dt.float32
+U32 = mybir.dt.uint32
+U8 = mybir.dt.uint8
+FP8X4 = mybir.dt.float8_e4m3fn_x4
+ALU = mybir.AluOpType
+
+P = 128
+PACK = 4
+CHUNK = 512
+NCHUNK = 4
+PLANE = 128
+
+
+def tile_selfspatialattentionmodule_pa_kernel(tc, x, W1, W2, out_0, out_1):
+    nc = tc.nc
+    x_d = x[0].rearrange("c h w -> c (h w)").rearrange("(p t) n -> p t n", t=PACK)
+    c1p_d = out_0[0].rearrange("(m p) i j -> p m (i j)", p=P)
+    c2_d = out_1[0].rearrange("(m p) h w -> p m (h w)", p=P)
+
+    with ExitStack() as ctx:
+        sb = ctx.enter_context(tc.tile_pool(name="sb", bufs=1))
+        ps_c1 = ctx.enter_context(tc.psum_pool(name="ps_c1", bufs=3))
+        ps_c2 = ctx.enter_context(tc.psum_pool(name="ps_c2", bufs=3))
+        ps_sum = ctx.enter_context(tc.psum_pool(name="ps_sum", bufs=2))
+
+        ident = sb.tile([P, P], F32, name="ident")
+        masks.make_identity(nc, ident[:])
+
+        xr = [sb.tile([P, PACK, CHUNK], BF16, name="xr%d" % c) for c in range(NCHUNK)]
+        wr = [sb.tile([P, 2 * 512], BF16, name="wr%d" % i) for i in range(2)]
+
+        def load_x(c):
+            nc.sync.dma_start(out=xr[c][:], in_=x_d[:, :, c * CHUNK : (c + 1) * CHUNK])
+
+        load_x(0)
+        for i, w in enumerate((W1, W2)):
+            nc.sync.dma_start(
+                out=wr[i][:].rearrange("p (t k) -> p t k", t=2),
+                in_=w.rearrange("(t p) k -> p t k", p=P),
+            )
+        for c in range(1, NCHUNK):
+            load_x(c)
+
+        xg = [sb.tile([P, PACK * CHUNK], BF16, name="xg%d" % c, align_bytes=64) for c in range(NCHUNK)]
+        xq = [sb.tile([P, CHUNK], U32, name="xq%d" % c, align_bytes=64) for c in range(NCHUNK)]
+        xs = [sb.tile([P, CHUNK], U8, name="xs%d" % c, align_bytes=64) for c in range(NCHUNK)]
+        wg = [sb.tile([P, PACK * 256], BF16, name="wg%d" % i, align_bytes=64) for i in range(2)]
+        wq = [sb.tile([P, 256], U32, name="wq%d" % i, align_bytes=64) for i in range(2)]
+        ws = [sb.tile([P, 256], U8, name="ws%d" % i, align_bytes=64) for i in range(2)]
+
+        def regroup(c):
+            dst = xg[c][:].rearrange("p (a b i j t) -> p a b i j t", a=2, b=2, i=8, j=16, t=PACK)
+            src = xr[c][:].rearrange("p t (i a j b) -> p a b i j t", i=8, a=2, j=16, b=2)
+            nc.vector.tensor_copy(out=dst[:, :, 0], in_=src[:, :, 0])
+            for a in range(2):
+                nc.scalar.copy(out=dst[:, a, 1], in_=src[:, a, 1])
+
+        def quant_x(c):
+            nc.vector.quantize_mx(out=xq[c][:].bitcast(FP8X4), scales=xs[c][:], in_=xg[c][:])
+
+        def prep_w(i):
+            words = wr[i][:].bitcast(F32).rearrange("p (t q u) -> p t u q", t=2, u=2)
+            wt = ps_c2.tile([P, 2, 2, P], F32, name="wt%d" % i, tag="c2")
+            for t in range(2):
+                for u in range(2):
+                    nc.tensor.transpose(wt[:, t, u, :], words[:, t, u, :], ident[:])
+            nc.scalar.copy(
+                out=wg[i][:].bitcast(F32).rearrange("p (t o u) -> p t o u", t=2, u=2),
+                in_=wt[:].rearrange("p t u o -> p t o u"),
+            )
+            nc.vector.quantize_mx(out=wq[i][:].bitcast(FP8X4), scales=ws[i][:], in_=wg[i][:])
+
+        def mx(out, i, m, c, lo, n, start, stop):
+            nc.tensor.matmul_mx(
+                out=out,
+                lhsT=wq[i][:, m * P : (m + 1) * P].bitcast(FP8X4),
+                lhsT_scale=ws[i][:, m * P : (m + 1) * P],
+                rhs=xq[c][:, lo : lo + n].bitcast(FP8X4),
+                rhs_scale=xs[c][:, lo : lo + n],
+                start=start,
+                stop=stop,
+            )
+
+        def products(c):
+            c1 = [ps_c1.tile([P, CHUNK], F32, name="c1_%d_%d" % (c, m), tag="c1") for m in range(2)]
+            c2 = [ps_c2.tile([P, CHUNK], F32, name="c2_%d_%d" % (c, m), tag="c2") for m in range(2)]
+            sm = ps_sum.tile([P, 2, PLANE], F32, name="sm%d" % c, tag="sm")
+            for m in range(2):
+                mx(c1[m][:], 0, m, c, 0, CHUNK, True, True)
+            for m in range(2):
+                mx(c2[m][:], 1, m, c, 0, CHUNK, True, True)
+            for m in range(2):
+                for q in range(4):
+                    mx(sm[:, m, :], 0, m, c, q * PLANE, PLANE, q == 0, q == 3)
+            return c1, c2, sm
+
+        def finish(c, c1, c2, sm):
+            c1sb = sb.tile([P, 2, PLANE], F32, name="c1sb%d" % c)
+            for m in range(2):
+                top = sb.tile([P, PLANE], F32, name="top_%d_%d" % (c, m))
+                nc.vector.tensor_reduce(
+                    out=top[:],
+                    in_=c1[m][:].rearrange("p (q n) -> p n q", q=4),
+                    axis=mybir.AxisListType.X,
+                    op=ALU.max,
+                )
+                nc.vector.scalar_tensor_tensor(
+                    out=c1sb[:, m, :], in0=sm[:, m, :], scalar=0.25, in1=top[:], op0=ALU.mult, op1=ALU.add
+                )
+                c2sb = sb.tile([P, CHUNK], F32, name="c2sb_%d_%d" % (c, m))
+                dst = c2sb[:].rearrange("p (i a j b) -> p a i j b", i=8, a=2, j=16, b=2)
+                src = c2[m][:].rearrange("p (a b i j) -> p a i j b", a=2, b=2, i=8, j=16)
+                for a in range(2):
+                    nc.scalar.copy(out=dst[:, a], in_=src[:, a])
+                nc.sync.dma_start(out=c2_d[:, m, c * CHUNK : (c + 1) * CHUNK], in_=c2sb[:])
+            nc.sync.dma_start(out=c1p_d[:, :, c * PLANE : (c + 1) * PLANE], in_=c1sb[:])
+
+        regroup(0)
+        prep_w(0)
+        prep_w(1)
+        quant_x(0)
+        for c in range(NCHUNK):
+            if c + 1 < NCHUNK:
+                regroup(c + 1)
+            banks = products(c)
+            if c + 1 < NCHUNK:
+                quant_x(c + 1)
+            finish(c, *banks)

@@ -30,6 +30,7 @@ def tile_selfspatialattentionmodule_pa_kernel(tc, x, W1, W2, out_0, out_1):
         ps_c1 = ctx.enter_context(tc.psum_pool(name="ps_c1", bufs=3))
         ps_c2 = ctx.enter_context(tc.psum_pool(name="ps_c2", bufs=3))
         ps_sum = ctx.enter_context(tc.psum_pool(name="ps_sum", bufs=2))
+        ctx.enter_context(tc.manual_schedule())
 
         ident = sb.tile([P, P], F32, name="ident")
         masks.make_identity(nc, ident[:])
@@ -55,27 +56,44 @@ def tile_selfspatialattentionmodule_pa_kernel(tc, x, W1, W2, out_0, out_1):
         wg = [sb.tile([P, PACK * 256], BF16, name="wg%d" % i, align_bytes=64) for i in range(2)]
         wq = [sb.tile([P, 256], U32, name="wq%d" % i, align_bytes=64) for i in range(2)]
         ws = [sb.tile([P, 256], U8, name="ws%d" % i, align_bytes=64) for i in range(2)]
+        c1sb = [sb.tile([P, 2, PLANE], F32, name="c1sb%d" % c) for c in range(NCHUNK)]
+        c2sb = [[sb.tile([P, CHUNK], F32, name="c2sb_%d_%d" % (c, m)) for m in range(2)] for c in range(NCHUNK)]
+        top = [[sb.tile([P, PLANE], F32, name="top_%d_%d" % (c, m)) for m in range(2)] for c in range(NCHUNK)]
+        c1 = {}
+        c2 = {}
+        sm = {}
+        wt = {}
 
-        def regroup(c):
+        def views(c):
             dst = xg[c][:].rearrange("p (a b i j t) -> p a b i j t", a=2, b=2, i=8, j=16, t=PACK)
             src = xr[c][:].rearrange("p t (i a j b) -> p a b i j t", i=8, a=2, j=16, b=2)
+            return dst, src
+
+        def rg_v(c):
+            dst, src = views(c)
             nc.vector.tensor_copy(out=dst[:, :, 0], in_=src[:, :, 0])
-            for a in range(2):
-                nc.scalar.copy(out=dst[:, a, 1], in_=src[:, a, 1])
+
+        def rg_s(c, a):
+            dst, src = views(c)
+            nc.scalar.copy(out=dst[:, a, 1], in_=src[:, a, 1])
 
         def quant_x(c):
             nc.vector.quantize_mx(out=xq[c][:].bitcast(FP8X4), scales=xs[c][:], in_=xg[c][:])
 
-        def prep_w(i):
+        def w_transposes(i):
             words = wr[i][:].bitcast(F32).rearrange("p (t q u) -> p t u q", t=2, u=2)
-            wt = ps_c2.tile([P, 2, 2, P], F32, name="wt%d" % i, tag="c2")
+            wt[i] = ps_c2.tile([P, 2, 2, P], F32, name="wt%d" % i, tag="c2")
             for t in range(2):
                 for u in range(2):
-                    nc.tensor.transpose(wt[:, t, u, :], words[:, t, u, :], ident[:])
+                    nc.tensor.transpose(wt[i][:, t, u, :], words[:, t, u, :], ident[:])
+
+        def w_copy(i):
             nc.scalar.copy(
                 out=wg[i][:].bitcast(F32).rearrange("p (t o u) -> p t o u", t=2, u=2),
-                in_=wt[:].rearrange("p t u o -> p t o u"),
+                in_=wt[i][:].rearrange("p t u o -> p t o u"),
             )
+
+        def w_quant(i):
             nc.vector.quantize_mx(out=wq[i][:].bitcast(FP8X4), scales=ws[i][:], in_=wg[i][:])
 
         def mx(out, i, m, c, lo, n, start, stop):
@@ -89,48 +107,91 @@ def tile_selfspatialattentionmodule_pa_kernel(tc, x, W1, W2, out_0, out_1):
                 stop=stop,
             )
 
-        def products(c):
-            c1 = [ps_c1.tile([P, CHUNK], F32, name="c1_%d_%d" % (c, m), tag="c1") for m in range(2)]
-            c2 = [ps_c2.tile([P, CHUNK], F32, name="c2_%d_%d" % (c, m), tag="c2") for m in range(2)]
-            sm = ps_sum.tile([P, 2, PLANE], F32, name="sm%d" % c, tag="sm")
-            for m in range(2):
-                mx(c1[m][:], 0, m, c, 0, CHUNK, True, True)
-            for m in range(2):
-                mx(c2[m][:], 1, m, c, 0, CHUNK, True, True)
+        def mm_c1(c, m):
+            c1[c, m] = ps_c1.tile([P, CHUNK], F32, name="c1_%d_%d" % (c, m), tag="c1")
+            mx(c1[c, m][:], 0, m, c, 0, CHUNK, True, True)
+
+        def mm_c2(c, m):
+            c2[c, m] = ps_c2.tile([P, CHUNK], F32, name="c2_%d_%d" % (c, m), tag="c2")
+            mx(c2[c, m][:], 1, m, c, 0, CHUNK, True, True)
+
+        def mm_sum(c):
+            sm[c] = ps_sum.tile([P, 2, PLANE], F32, name="sm%d" % c, tag="sm")
             for m in range(2):
                 for q in range(4):
-                    mx(sm[:, m, :], 0, m, c, q * PLANE, PLANE, q == 0, q == 3)
-            return c1, c2, sm
+                    mx(sm[c][:, m, :], 0, m, c, q * PLANE, PLANE, q == 0, q == 3)
 
-        def finish(c, c1, c2, sm):
-            c1sb = sb.tile([P, 2, PLANE], F32, name="c1sb%d" % c)
-            for m in range(2):
-                top = sb.tile([P, PLANE], F32, name="top_%d_%d" % (c, m))
-                nc.vector.tensor_reduce(
-                    out=top[:],
-                    in_=c1[m][:].rearrange("p (q n) -> p n q", q=4),
-                    axis=mybir.AxisListType.X,
-                    op=ALU.max,
-                )
-                nc.vector.scalar_tensor_tensor(
-                    out=c1sb[:, m, :], in0=sm[:, m, :], scalar=0.25, in1=top[:], op0=ALU.mult, op1=ALU.add
-                )
-                c2sb = sb.tile([P, CHUNK], F32, name="c2sb_%d_%d" % (c, m))
-                dst = c2sb[:].rearrange("p (i a j b) -> p a i j b", i=8, a=2, j=16, b=2)
-                src = c2[m][:].rearrange("p (a b i j) -> p a i j b", a=2, b=2, i=8, j=16)
-                for a in range(2):
-                    nc.scalar.copy(out=dst[:, a], in_=src[:, a])
-                nc.sync.dma_start(out=c2_d[:, m, c * CHUNK : (c + 1) * CHUNK], in_=c2sb[:])
-            nc.sync.dma_start(out=c1p_d[:, :, c * PLANE : (c + 1) * PLANE], in_=c1sb[:])
+        def products(c):
+            mm_c1(c, 0)
+            mm_c2(c, 0)
+            mm_c1(c, 1)
+            mm_c2(c, 1)
+            mm_sum(c)
 
-        regroup(0)
-        prep_w(0)
-        prep_w(1)
+        def red(c, m):
+            nc.vector.tensor_reduce(
+                out=top[c][m][:],
+                in_=c1[c, m][:].rearrange("p (q n) -> p n q", q=4),
+                axis=mybir.AxisListType.X,
+                op=ALU.max,
+            )
+
+        def stt(c, m):
+            nc.vector.scalar_tensor_tensor(
+                out=c1sb[c][:, m, :], in0=sm[c][:, m, :], scalar=0.25, in1=top[c][m][:], op0=ALU.mult, op1=ALU.add
+            )
+
+        def store_c1(c):
+            nc.sync.dma_start(out=c1p_d[:, :, c * PLANE : (c + 1) * PLANE], in_=c1sb[c][:])
+
+        def ev(c, m):
+            dst = c2sb[c][m][:].rearrange("p (i a j b) -> p a i j b", i=8, a=2, j=16, b=2)
+            src = c2[c, m][:].rearrange("p (a b i j) -> p a i j b", a=2, b=2, i=8, j=16)
+            for a in range(2):
+                nc.scalar.copy(out=dst[:, a], in_=src[:, a])
+            nc.sync.dma_start(out=c2_d[:, m, c * CHUNK : (c + 1) * CHUNK], in_=c2sb[c][m][:])
+
+        rg_v(0)
+        rg_s(0, 0)
+        rg_s(0, 1)
+        w_transposes(0)
+        w_transposes(1)
+        w_copy(0)
+        w_copy(1)
         quant_x(0)
-        for c in range(NCHUNK):
-            if c + 1 < NCHUNK:
-                regroup(c + 1)
-            banks = products(c)
-            if c + 1 < NCHUNK:
-                quant_x(c + 1)
-            finish(c, *banks)
+        w_quant(0)
+        w_quant(1)
+        products(0)
+        rg_v(1)
+        rg_s(1, 0)
+        rg_s(1, 1)
+        red(0, 0)
+        quant_x(1)
+        ev(0, 0)
+        products(1)
+        rg_v(2)
+        rg_s(2, 0)
+        rg_s(2, 1)
+        red(0, 1)
+        quant_x(2)
+        stt(0, 0)
+        stt(0, 1)
+        store_c1(0)
+        ev(0, 1)
+        products(2)
+        rg_v(3)
+        rg_s(3, 0)
+        rg_s(3, 1)
+        red(1, 0)
+        quant_x(3)
+        for c in range(1, NCHUNK):
+            if c > 1:
+                red(c, 0)
+            ev(c, 0)
+            red(c, 1)
+            ev(c, 1)
+            if c + 2 < NCHUNK:
+                products(c + 2)
+            stt(c, 0)
+            stt(c, 1)
+            store_c1(c)

@@ -18,7 +18,6 @@ CHUNK = 512
 NCHUNK = 4
 PLANE = 128
 
-
 def tile_selfspatialattentionmodule_pa_kernel(tc, x, W1, W2, out_0, out_1):
     nc = tc.nc
     x_d = x[0].rearrange("c h w -> c (h w)").rearrange("(p t) n -> p t n", t=PACK)
@@ -65,17 +64,17 @@ def tile_selfspatialattentionmodule_pa_kernel(tc, x, W1, W2, out_0, out_1):
         wt = {}
 
         def views(c):
-            dst = xg[c][:].rearrange("p (a b i j t) -> p a b i j t", a=2, b=2, i=8, j=16, t=PACK)
-            src = xr[c][:].rearrange("p t (i a j b) -> p a b i j t", i=8, a=2, j=16, b=2)
+            dst = xg[c][:].rearrange("p (a b i g s t) -> p a b i g t s", a=2, b=2, i=8, g=4, s=4, t=PACK)
+            src = xr[c][:].rearrange("p t (i a g s b) -> p a b i g t s", i=8, a=2, g=4, s=4, b=2)
             return dst, src
 
-        def rg_v(c):
+        def rg_v(c, a, b):
             dst, src = views(c)
-            nc.vector.tensor_copy(out=dst[:, :, 0], in_=src[:, :, 0])
+            nc.vector.tensor_copy(out=dst[:, a, b], in_=src[:, a, b])
 
-        def rg_s(c, a):
+        def rg_s(c, a, b):
             dst, src = views(c)
-            nc.scalar.copy(out=dst[:, a, 1], in_=src[:, a, 1])
+            nc.scalar.copy(out=dst[:, a, b], in_=src[:, a, b])
 
         def quant_x(c):
             nc.vector.quantize_mx(out=xq[c][:].bitcast(FP8X4), scales=xs[c][:], in_=xg[c][:])
@@ -147,13 +146,20 @@ def tile_selfspatialattentionmodule_pa_kernel(tc, x, W1, W2, out_0, out_1):
         def ev(c, m):
             dst = c2sb[c][m][:].rearrange("p (i a j b) -> p a i j b", i=8, a=2, j=16, b=2)
             src = c2[c, m][:].rearrange("p (a b i j) -> p a i j b", a=2, b=2, i=8, j=16)
-            for a in range(2):
-                nc.scalar.copy(out=dst[:, a], in_=src[:, a])
+            nc.scalar.copy(out=dst, in_=src)
             nc.sync.dma_start(out=c2_d[:, m, c * CHUNK : (c + 1) * CHUNK], in_=c2sb[c][m][:])
 
-        rg_v(0)
-        rg_s(0, 0)
-        rg_s(0, 1)
+        PLANES = ((0, 0), (1, 0), (0, 1), (1, 1))
+        V_SHARE = (2, 2, 2, 1)
+
+        def regroup(c):
+            for k, (a, b) in enumerate(PLANES):
+                if k < V_SHARE[c]:
+                    rg_v(c, a, b)
+                else:
+                    rg_s(c, a, b)
+
+        regroup(0)
         w_transposes(0)
         w_transposes(1)
         w_copy(0)
@@ -162,36 +168,17 @@ def tile_selfspatialattentionmodule_pa_kernel(tc, x, W1, W2, out_0, out_1):
         w_quant(0)
         w_quant(1)
         products(0)
-        rg_v(1)
-        rg_s(1, 0)
-        rg_s(1, 1)
-        red(0, 0)
-        quant_x(1)
-        ev(0, 0)
-        products(1)
-        rg_v(2)
-        rg_s(2, 0)
-        rg_s(2, 1)
-        red(0, 1)
-        quant_x(2)
-        stt(0, 0)
-        stt(0, 1)
-        store_c1(0)
-        ev(0, 1)
-        products(2)
-        rg_v(3)
-        rg_s(3, 0)
-        rg_s(3, 1)
-        red(1, 0)
-        quant_x(3)
-        for c in range(1, NCHUNK):
-            if c > 1:
-                red(c, 0)
+        for c in range(NCHUNK):
+            if c + 1 < NCHUNK:
+                regroup(c + 1)
+            red(c, 0)
+            if c + 1 < NCHUNK:
+                quant_x(c + 1)
             ev(c, 0)
             red(c, 1)
             ev(c, 1)
-            if c + 2 < NCHUNK:
-                products(c + 2)
+            if c + 1 < NCHUNK:
+                products(c + 1)
             stt(c, 0)
             stt(c, 1)
             store_c1(c)

@@ -18,6 +18,7 @@ CHUNK = 512
 NCHUNK = 4
 PLANE = 128
 
+
 def tile_selfspatialattentionmodule_pa_kernel(tc, x, W1, W2, out_0, out_1):
     nc = tc.nc
     x_d = x[0].rearrange("c h w -> c (h w)").rearrange("(p t) n -> p t n", t=PACK)
@@ -43,8 +44,8 @@ def tile_selfspatialattentionmodule_pa_kernel(tc, x, W1, W2, out_0, out_1):
         load_x(0)
         for i, w in enumerate((W1, W2)):
             nc.sync.dma_start(
-                out=wr[i][:].rearrange("p (t k) -> p t k", t=2),
-                in_=w.rearrange("(t p) k -> p t k", p=P),
+                out=wr[i][:].rearrange("p (m k) -> p m k", m=2),
+                in_=w.rearrange("(m p) k -> p m k", p=P),
             )
         for c in range(1, NCHUNK):
             load_x(c)
@@ -52,133 +53,105 @@ def tile_selfspatialattentionmodule_pa_kernel(tc, x, W1, W2, out_0, out_1):
         xg = [sb.tile([P, PACK * CHUNK], BF16, name="xg%d" % c, align_bytes=64) for c in range(NCHUNK)]
         xq = [sb.tile([P, CHUNK], U32, name="xq%d" % c, align_bytes=64) for c in range(NCHUNK)]
         xs = [sb.tile([P, CHUNK], U8, name="xs%d" % c, align_bytes=64) for c in range(NCHUNK)]
-        wg = [sb.tile([P, PACK * 256], BF16, name="wg%d" % i, align_bytes=64) for i in range(2)]
-        wq = [sb.tile([P, 256], U32, name="wq%d" % i, align_bytes=64) for i in range(2)]
-        ws = [sb.tile([P, 256], U8, name="ws%d" % i, align_bytes=64) for i in range(2)]
+        wg = [[sb.tile([P, PACK * P], BF16, name="wg_%d_%d" % (i, m), align_bytes=64) for m in range(2)] for i in range(2)]
+        wq = [[sb.tile([P, P], U32, name="wq_%d_%d" % (i, m), align_bytes=64) for m in range(2)] for i in range(2)]
+        ws = [[sb.tile([P, P], U8, name="ws_%d_%d" % (i, m), align_bytes=64) for m in range(2)] for i in range(2)]
+        top = [sb.tile([P, 2, PLANE], F32, name="top%d" % c) for c in range(NCHUNK)]
         c1sb = [sb.tile([P, 2, PLANE], F32, name="c1sb%d" % c) for c in range(NCHUNK)]
         c2sb = [[sb.tile([P, CHUNK], F32, name="c2sb_%d_%d" % (c, m)) for m in range(2)] for c in range(NCHUNK)]
-        top = [[sb.tile([P, PLANE], F32, name="top_%d_%d" % (c, m)) for m in range(2)] for c in range(NCHUNK)]
+        wt = {}
         c1 = {}
         c2 = {}
         sm = {}
-        wt = {}
 
-        def views(c):
-            dst = xg[c][:].rearrange("p (a b i g s t) -> p a b i g t s", a=2, b=2, i=8, g=4, s=4, t=PACK)
-            src = xr[c][:].rearrange("p t (i a g s b) -> p a b i g t s", i=8, a=2, g=4, s=4, b=2)
-            return dst, src
+        def regroup(c):
+            dst = xg[c][:].rearrange("p (a b i j t) -> p a b i j t", a=2, b=2, i=8, j=16, t=PACK)
+            src = xr[c][:].rearrange("p t (i a j b) -> p a b i j t", i=8, a=2, j=16, b=2)
+            nc.vector.tensor_copy(out=dst[:, :, 0], in_=src[:, :, 0])
+            for a in range(2):
+                nc.scalar.copy(out=dst[:, a, 1], in_=src[:, a, 1])
 
-        def rg_v(c, a, b):
-            dst, src = views(c)
-            nc.vector.tensor_copy(out=dst[:, a, b], in_=src[:, a, b])
-
-        def rg_s(c, a, b):
-            dst, src = views(c)
-            nc.scalar.copy(out=dst[:, a, b], in_=src[:, a, b])
-
-        def quant_x(c):
+        def quantise_x(c):
             nc.vector.quantize_mx(out=xq[c][:].bitcast(FP8X4), scales=xs[c][:], in_=xg[c][:])
 
-        def w_transposes(i):
-            words = wr[i][:].bitcast(F32).rearrange("p (t q u) -> p t u q", t=2, u=2)
-            wt[i] = ps_c2.tile([P, 2, 2, P], F32, name="wt%d" % i, tag="c2")
-            for t in range(2):
-                for u in range(2):
-                    nc.tensor.transpose(wt[i][:, t, u, :], words[:, t, u, :], ident[:])
+        def transpose_w(i, m):
+            words = wr[i][:].bitcast(F32).rearrange("p (m q u) -> p m u q", m=2, u=2)
+            wt[i, m] = ps_c2.tile([P, 2, P], F32, name="wt_%d_%d" % (i, m), tag="c2")
+            for u in range(2):
+                nc.tensor.transpose(wt[i, m][:, u, :], words[:, m, u, :], ident[:])
 
-        def w_copy(i):
+        def copy_w(i, m):
             nc.scalar.copy(
-                out=wg[i][:].bitcast(F32).rearrange("p (t o u) -> p t o u", t=2, u=2),
-                in_=wt[i][:].rearrange("p t u o -> p t o u"),
+                out=wg[i][m][:].bitcast(F32).rearrange("p (o u) -> p o u", u=2),
+                in_=wt[i, m][:].rearrange("p u o -> p o u"),
             )
 
-        def w_quant(i):
-            nc.vector.quantize_mx(out=wq[i][:].bitcast(FP8X4), scales=ws[i][:], in_=wg[i][:])
+        def quantise_w(i, m):
+            nc.vector.quantize_mx(out=wq[i][m][:].bitcast(FP8X4), scales=ws[i][m][:], in_=wg[i][m][:])
 
-        def mx(out, i, m, c, lo, n, start, stop):
+        def mx_pass(out, i, m, c, first, width, start, stop):
             nc.tensor.matmul_mx(
                 out=out,
-                lhsT=wq[i][:, m * P : (m + 1) * P].bitcast(FP8X4),
-                lhsT_scale=ws[i][:, m * P : (m + 1) * P],
-                rhs=xq[c][:, lo : lo + n].bitcast(FP8X4),
-                rhs_scale=xs[c][:, lo : lo + n],
+                lhsT=wq[i][m][:].bitcast(FP8X4),
+                lhsT_scale=ws[i][m][:],
+                rhs=xq[c][:, first : first + width].bitcast(FP8X4),
+                rhs_scale=xs[c][:, first : first + width],
                 start=start,
                 stop=stop,
             )
 
-        def mm_c1(c, m):
-            c1[c, m] = ps_c1.tile([P, CHUNK], F32, name="c1_%d_%d" % (c, m), tag="c1")
-            mx(c1[c, m][:], 0, m, c, 0, CHUNK, True, True)
-
-        def mm_c2(c, m):
-            c2[c, m] = ps_c2.tile([P, CHUNK], F32, name="c2_%d_%d" % (c, m), tag="c2")
-            mx(c2[c, m][:], 1, m, c, 0, CHUNK, True, True)
-
-        def mm_sum(c):
+        def products(c):
             sm[c] = ps_sum.tile([P, 2, PLANE], F32, name="sm%d" % c, tag="sm")
             for m in range(2):
+                c1[c, m] = ps_c1.tile([P, CHUNK], F32, name="c1_%d_%d" % (c, m), tag="c1")
+                c2[c, m] = ps_c2.tile([P, CHUNK], F32, name="c2_%d_%d" % (c, m), tag="c2")
+                mx_pass(c1[c, m][:], 0, m, c, 0, CHUNK, True, True)
+                mx_pass(c2[c, m][:], 1, m, c, 0, CHUNK, True, True)
+            for m in range(2):
                 for q in range(4):
-                    mx(sm[c][:, m, :], 0, m, c, q * PLANE, PLANE, q == 0, q == 3)
+                    mx_pass(sm[c][:, m, :], 0, m, c, q * PLANE, PLANE, q == 0, q == 3)
 
-        def products(c):
-            mm_c1(c, 0)
-            mm_c2(c, 0)
-            mm_c1(c, 1)
-            mm_c2(c, 1)
-            mm_sum(c)
-
-        def red(c, m):
+        def window_max(c, m):
             nc.vector.tensor_reduce(
-                out=top[c][m][:],
+                out=top[c][:, m, :],
                 in_=c1[c, m][:].rearrange("p (q n) -> p n q", q=4),
                 axis=mybir.AxisListType.X,
                 op=ALU.max,
             )
 
-        def stt(c, m):
+        def finish_c1(c):
             nc.vector.scalar_tensor_tensor(
-                out=c1sb[c][:, m, :], in0=sm[c][:, m, :], scalar=0.25, in1=top[c][m][:], op0=ALU.mult, op1=ALU.add
+                out=c1sb[c][:], in0=sm[c][:], scalar=0.25, in1=top[c][:], op0=ALU.mult, op1=ALU.add
             )
-
-        def store_c1(c):
             nc.sync.dma_start(out=c1p_d[:, :, c * PLANE : (c + 1) * PLANE], in_=c1sb[c][:])
 
-        def ev(c, m):
-            dst = c2sb[c][m][:].rearrange("p (i a j b) -> p a i j b", i=8, a=2, j=16, b=2)
-            src = c2[c, m][:].rearrange("p (a b i j) -> p a i j b", a=2, b=2, i=8, j=16)
-            nc.scalar.copy(out=dst, in_=src)
+        def finish_c2(c, m):
+            nc.scalar.copy(
+                out=c2sb[c][m][:].rearrange("p (i a j b) -> p a i j b", i=8, a=2, j=16, b=2),
+                in_=c2[c, m][:].rearrange("p (a b i j) -> p a i j b", a=2, b=2, i=8, j=16),
+            )
             nc.sync.dma_start(out=c2_d[:, m, c * CHUNK : (c + 1) * CHUNK], in_=c2sb[c][m][:])
 
-        PLANES = ((0, 0), (1, 0), (0, 1), (1, 1))
-        V_SHARE = (2, 2, 2, 1)
-
-        def regroup(c):
-            for k, (a, b) in enumerate(PLANES):
-                if k < V_SHARE[c]:
-                    rg_v(c, a, b)
-                else:
-                    rg_s(c, a, b)
-
+        tiles = [(i, m) for i in range(2) for m in range(2)]
         regroup(0)
-        w_transposes(0)
-        w_transposes(1)
-        w_copy(0)
-        w_copy(1)
-        quant_x(0)
-        w_quant(0)
-        w_quant(1)
+        for i, m in tiles:
+            transpose_w(i, m)
+        for i, m in tiles:
+            copy_w(i, m)
+        quantise_x(0)
+        for i, m in tiles:
+            quantise_w(i, m)
         products(0)
         for c in range(NCHUNK):
-            if c + 1 < NCHUNK:
+            more = c + 1 < NCHUNK
+            if more:
                 regroup(c + 1)
-            red(c, 0)
-            if c + 1 < NCHUNK:
-                quant_x(c + 1)
-            ev(c, 0)
-            red(c, 1)
-            ev(c, 1)
-            if c + 1 < NCHUNK:
+            window_max(c, 0)
+            if more:
+                quantise_x(c + 1)
+            finish_c2(c, 0)
+            window_max(c, 1)
+            finish_c2(c, 1)
+            if more:
                 products(c + 1)
-            stt(c, 0)
-            stt(c, 1)
-            store_c1(c)
+            finish_c1(c)

@@ -14,16 +14,19 @@ ALU = mybir.AluOpType
 
 P = 128
 PACK = 4
+K = P * PACK
 CHUNK = 512
-NCHUNK = 4
-PLANE = 128
+N_CHUNKS = 4
+PLANE = CHUNK // 4
+ALIGN = 64
 
 
 def tile_selfspatialattentionmodule_pa_kernel(tc, x, W1, W2, out_0, out_1):
     nc = tc.nc
-    x_d = x[0].rearrange("c h w -> c (h w)").rearrange("(p t) n -> p t n", t=PACK)
-    c1p_d = out_0[0].rearrange("(m p) i j -> p m (i j)", p=P)
-    c2_d = out_1[0].rearrange("(m p) h w -> p m (h w)", p=P)
+    x_rows = x[0].rearrange("c h w -> c (h w)").rearrange("(p t) n -> p t n", t=PACK)
+    c1p_out = out_0[0].rearrange("(m p) i j -> p m (i j)", p=P)
+    c2_out = out_1[0].rearrange("(m p) h w -> p m (h w)", p=P)
+    weight_tiles = [(w, m) for w in range(2) for m in range(2)]
 
     with ExitStack() as ctx:
         sb = ctx.enter_context(tc.tile_pool(name="sb", bufs=1))
@@ -32,68 +35,68 @@ def tile_selfspatialattentionmodule_pa_kernel(tc, x, W1, W2, out_0, out_1):
         ps_sum = ctx.enter_context(tc.psum_pool(name="ps_sum", bufs=2))
         ctx.enter_context(tc.manual_schedule())
 
-        ident = sb.tile([P, P], F32, name="ident")
-        masks.make_identity(nc, ident[:])
+        identity = sb.tile([P, P], F32, name="identity")
+        masks.make_identity(nc, identity[:])
 
-        xr = [sb.tile([P, PACK, CHUNK], BF16, name="xr%d" % c) for c in range(NCHUNK)]
-        wr = [sb.tile([P, 2 * 512], BF16, name="wr%d" % i) for i in range(2)]
+        xr = [sb.tile([P, PACK, CHUNK], BF16, name="xr%d" % c) for c in range(N_CHUNKS)]
+        wr = [sb.tile([P, 2 * K], BF16, name="wr%d" % w) for w in range(2)]
 
         def load_x(c):
-            nc.sync.dma_start(out=xr[c][:], in_=x_d[:, :, c * CHUNK : (c + 1) * CHUNK])
+            nc.sync.dma_start(out=xr[c][:], in_=x_rows[:, :, c * CHUNK : (c + 1) * CHUNK])
 
         load_x(0)
-        for i, w in enumerate((W1, W2)):
+        for w, weights in enumerate((W1, W2)):
             nc.sync.dma_start(
-                out=wr[i][:].rearrange("p (m k) -> p m k", m=2),
-                in_=w.rearrange("(m p) k -> p m k", p=P),
+                out=wr[w][:].rearrange("p (m k) -> p m k", m=2),
+                in_=weights.rearrange("(m p) k -> p m k", p=P),
             )
-        for c in range(1, NCHUNK):
+        for c in range(1, N_CHUNKS):
             load_x(c)
 
-        xg = [sb.tile([P, PACK * CHUNK], BF16, name="xg%d" % c, align_bytes=64) for c in range(NCHUNK)]
-        xq = [sb.tile([P, CHUNK], U32, name="xq%d" % c, align_bytes=64) for c in range(NCHUNK)]
-        xs = [sb.tile([P, CHUNK], U8, name="xs%d" % c, align_bytes=64) for c in range(NCHUNK)]
-        wg = [[sb.tile([P, PACK * P], BF16, name="wg_%d_%d" % (i, m), align_bytes=64) for m in range(2)] for i in range(2)]
-        wq = [[sb.tile([P, P], U32, name="wq_%d_%d" % (i, m), align_bytes=64) for m in range(2)] for i in range(2)]
-        ws = [[sb.tile([P, P], U8, name="ws_%d_%d" % (i, m), align_bytes=64) for m in range(2)] for i in range(2)]
-        top = [sb.tile([P, 2, PLANE], F32, name="top%d" % c) for c in range(NCHUNK)]
-        c1sb = [sb.tile([P, 2, PLANE], F32, name="c1sb%d" % c) for c in range(NCHUNK)]
-        c2sb = [[sb.tile([P, CHUNK], F32, name="c2sb_%d_%d" % (c, m)) for m in range(2)] for c in range(NCHUNK)]
+        xg = [sb.tile([P, CHUNK * PACK], BF16, name="xg%d" % c, align_bytes=ALIGN) for c in range(N_CHUNKS)]
+        xq = [sb.tile([P, CHUNK], U32, name="xq%d" % c, align_bytes=ALIGN) for c in range(N_CHUNKS)]
+        xs = [sb.tile([P, CHUNK], U8, name="xs%d" % c, align_bytes=ALIGN) for c in range(N_CHUNKS)]
+        wg = {wm: sb.tile([P, P * PACK], BF16, name="wg_%d_%d" % wm, align_bytes=ALIGN) for wm in weight_tiles}
+        wq = {wm: sb.tile([P, P], U32, name="wq_%d_%d" % wm, align_bytes=ALIGN) for wm in weight_tiles}
+        ws = {wm: sb.tile([P, P], U8, name="ws_%d_%d" % wm, align_bytes=ALIGN) for wm in weight_tiles}
+        top = [sb.tile([P, 2, PLANE], F32, name="top%d" % c) for c in range(N_CHUNKS)]
+        c1p_sb = [sb.tile([P, 2, PLANE], F32, name="c1p_sb%d" % c) for c in range(N_CHUNKS)]
+        c2_sb = {(c, m): sb.tile([P, CHUNK], F32, name="c2_sb_%d_%d" % (c, m)) for c in range(N_CHUNKS) for m in range(2)}
         wt = {}
         c1 = {}
         c2 = {}
-        sm = {}
+        sums = {}
+
+        def transpose_w(w, m):
+            words = wr[w][:].bitcast(F32).rearrange("p (m q u) -> p m u q", m=2, u=2)
+            wt[w, m] = ps_c2.tile([P, 2, P], F32, name="wt_%d_%d" % (w, m), tag="c2")
+            for u in range(2):
+                nc.tensor.transpose(wt[w, m][:, u, :], words[:, m, u, :], identity[:])
+
+        def copy_w(w, m):
+            nc.scalar.copy(
+                out=wg[w, m][:].bitcast(F32).rearrange("p (o u) -> p o u", u=2),
+                in_=wt[w, m][:].rearrange("p u o -> p o u"),
+            )
+
+        def quantise_w(w, m):
+            nc.vector.quantize_mx(out=wq[w, m][:].bitcast(FP8X4), scales=ws[w, m][:], in_=wg[w, m][:])
 
         def regroup(c):
-            dst = xg[c][:].rearrange("p (a b i j t) -> p a b i j t", a=2, b=2, i=8, j=16, t=PACK)
-            src = xr[c][:].rearrange("p t (i a j b) -> p a b i j t", i=8, a=2, j=16, b=2)
-            nc.vector.tensor_copy(out=dst[:, :, 0], in_=src[:, :, 0])
+            words = xg[c][:].rearrange("p (a b i g s t) -> p a b i g t s", a=2, b=2, i=8, g=4, s=4, t=PACK)
+            rows = xr[c][:].rearrange("p t (i a g s b) -> p a b i g t s", i=8, a=2, g=4, s=4, b=2)
             for a in range(2):
-                nc.scalar.copy(out=dst[:, a, 1], in_=src[:, a, 1])
+                nc.vector.tensor_copy(out=words[:, a, 0], in_=rows[:, a, 0])
+                nc.scalar.copy(out=words[:, a, 1], in_=rows[:, a, 1])
 
         def quantise_x(c):
             nc.vector.quantize_mx(out=xq[c][:].bitcast(FP8X4), scales=xs[c][:], in_=xg[c][:])
 
-        def transpose_w(i, m):
-            words = wr[i][:].bitcast(F32).rearrange("p (m q u) -> p m u q", m=2, u=2)
-            wt[i, m] = ps_c2.tile([P, 2, P], F32, name="wt_%d_%d" % (i, m), tag="c2")
-            for u in range(2):
-                nc.tensor.transpose(wt[i, m][:, u, :], words[:, m, u, :], ident[:])
-
-        def copy_w(i, m):
-            nc.scalar.copy(
-                out=wg[i][m][:].bitcast(F32).rearrange("p (o u) -> p o u", u=2),
-                in_=wt[i, m][:].rearrange("p u o -> p o u"),
-            )
-
-        def quantise_w(i, m):
-            nc.vector.quantize_mx(out=wq[i][m][:].bitcast(FP8X4), scales=ws[i][m][:], in_=wg[i][m][:])
-
-        def mx_pass(out, i, m, c, first, width, start, stop):
+        def mx_pass(out, w, m, c, first, width, start, stop):
             nc.tensor.matmul_mx(
                 out=out,
-                lhsT=wq[i][m][:].bitcast(FP8X4),
-                lhsT_scale=ws[i][m][:],
+                lhsT=wq[w, m][:].bitcast(FP8X4),
+                lhsT_scale=ws[w, m][:],
                 rhs=xq[c][:, first : first + width].bitcast(FP8X4),
                 rhs_scale=xs[c][:, first : first + width],
                 start=start,
@@ -101,57 +104,59 @@ def tile_selfspatialattentionmodule_pa_kernel(tc, x, W1, W2, out_0, out_1):
             )
 
         def products(c):
-            sm[c] = ps_sum.tile([P, 2, PLANE], F32, name="sm%d" % c, tag="sm")
+            sums[c] = ps_sum.tile([P, 2, PLANE], F32, name="sums%d" % c, tag="sums")
             for m in range(2):
                 c1[c, m] = ps_c1.tile([P, CHUNK], F32, name="c1_%d_%d" % (c, m), tag="c1")
                 c2[c, m] = ps_c2.tile([P, CHUNK], F32, name="c2_%d_%d" % (c, m), tag="c2")
                 mx_pass(c1[c, m][:], 0, m, c, 0, CHUNK, True, True)
                 mx_pass(c2[c, m][:], 1, m, c, 0, CHUNK, True, True)
             for m in range(2):
-                for q in range(4):
-                    mx_pass(sm[c][:, m, :], 0, m, c, q * PLANE, PLANE, q == 0, q == 3)
+                for place in range(4):
+                    mx_pass(sums[c][:, m, :], 0, m, c, place * PLANE, PLANE, place == 0, place == 3)
 
         def window_max(c, m):
             nc.vector.tensor_reduce(
                 out=top[c][:, m, :],
-                in_=c1[c, m][:].rearrange("p (q n) -> p n q", q=4),
+                in_=c1[c, m][:].rearrange("p (place n) -> p n place", place=4),
                 axis=mybir.AxisListType.X,
                 op=ALU.max,
             )
 
-        def finish_c1(c):
+        def add_mean(c, m):
             nc.vector.scalar_tensor_tensor(
-                out=c1sb[c][:], in0=sm[c][:], scalar=0.25, in1=top[c][:], op0=ALU.mult, op1=ALU.add
+                out=c1p_sb[c][:, m, :], in0=sums[c][:, m, :], scalar=0.25, in1=top[c][:, m, :], op0=ALU.mult, op1=ALU.add
             )
-            nc.sync.dma_start(out=c1p_d[:, :, c * PLANE : (c + 1) * PLANE], in_=c1sb[c][:])
+
+        def store_c1p(c):
+            nc.sync.dma_start(out=c1p_out[:, :, c * PLANE : (c + 1) * PLANE], in_=c1p_sb[c][:])
 
         def finish_c2(c, m):
             nc.scalar.copy(
-                out=c2sb[c][m][:].rearrange("p (i a j b) -> p a i j b", i=8, a=2, j=16, b=2),
+                out=c2_sb[c, m][:].rearrange("p (i a j b) -> p a i j b", i=8, a=2, j=16, b=2),
                 in_=c2[c, m][:].rearrange("p (a b i j) -> p a i j b", a=2, b=2, i=8, j=16),
             )
-            nc.sync.dma_start(out=c2_d[:, m, c * CHUNK : (c + 1) * CHUNK], in_=c2sb[c][m][:])
+            nc.sync.dma_start(out=c2_out[:, m, c * CHUNK : (c + 1) * CHUNK], in_=c2_sb[c, m][:])
 
-        tiles = [(i, m) for i in range(2) for m in range(2)]
         regroup(0)
-        for i, m in tiles:
-            transpose_w(i, m)
-        for i, m in tiles:
-            copy_w(i, m)
+        for w, m in weight_tiles:
+            transpose_w(w, m)
+        for w, m in weight_tiles:
+            copy_w(w, m)
         quantise_x(0)
-        for i, m in tiles:
-            quantise_w(i, m)
+        for w, m in weight_tiles:
+            quantise_w(w, m)
         products(0)
-        for c in range(NCHUNK):
-            more = c + 1 < NCHUNK
-            if more:
+        for c in range(N_CHUNKS):
+            if c + 1 < N_CHUNKS:
                 regroup(c + 1)
             window_max(c, 0)
-            if more:
+            if c + 1 < N_CHUNKS:
                 quantise_x(c + 1)
             finish_c2(c, 0)
             window_max(c, 1)
             finish_c2(c, 1)
-            if more:
+            if c + 1 < N_CHUNKS:
                 products(c + 1)
-            finish_c1(c)
+            add_mean(c, 0)
+            add_mean(c, 1)
+            store_c1p(c)

@@ -83,8 +83,8 @@ def tile_selfspatialattentionmodule_pa_kernel(tc, x, W1, W2, out_0, out_1):
             nc.vector.quantize_mx(out=wq[w, m][:].bitcast(FP8X4), scales=ws[w, m][:], in_=wg[w, m][:])
 
         def regroup(c):
-            words = xg[c][:].rearrange("p (a b i g s t) -> p a b i g t s", a=2, b=2, i=8, g=4, s=4, t=PACK)
-            rows = xr[c][:].rearrange("p t (i a g s b) -> p a b i g t s", i=8, a=2, g=4, s=4, b=2)
+            words = xg[c][:].rearrange("p (a b i j t) -> p a b i j t", a=2, b=2, i=8, j=16, t=PACK)
+            rows = xr[c][:].rearrange("p t (i a j b) -> p a b i j t", i=8, a=2, j=16, b=2)
             for a in range(2):
                 nc.vector.tensor_copy(out=words[:, a, 0], in_=rows[:, a, 0])
                 nc.scalar.copy(out=words[:, a, 1], in_=rows[:, a, 1])

@@ -17,16 +17,19 @@ PACK = 4
 K = P * PACK
 CHUNK = 512
 N_CHUNKS = 4
-PLANE = CHUNK // 4
+WIN_ROWS = 8
+WIN_COLS = 16
+PLANE = WIN_ROWS * WIN_COLS
+RUN = 4
 ALIGN = 64
 
 
 def tile_selfspatialattentionmodule_pa_kernel(tc, x, W1, W2, out_0, out_1):
     nc = tc.nc
-    x_rows = x[0].rearrange("c h w -> c (h w)").rearrange("(p t) n -> p t n", t=PACK)
-    c1p_out = out_0[0].rearrange("(m p) i j -> p m (i j)", p=P)
+    x_rows = x[0].rearrange("k h w -> k (h w)").rearrange("(p t) pixel -> p t pixel", t=PACK)
+    c1p_out = out_0[0].rearrange("(m p) row col -> p m (row col)", p=P)
     c2_out = out_1[0].rearrange("(m p) h w -> p m (h w)", p=P)
-    weight_tiles = [(w, m) for w in range(2) for m in range(2)]
+    weight_tiles = [(mat, m) for mat in range(2) for m in range(2)]
 
     with ExitStack() as ctx:
         sb = ctx.enter_context(tc.tile_pool(name="sb", bufs=1))
@@ -39,15 +42,15 @@ def tile_selfspatialattentionmodule_pa_kernel(tc, x, W1, W2, out_0, out_1):
         masks.make_identity(nc, identity[:])
 
         xr = [sb.tile([P, PACK, CHUNK], BF16, name="xr%d" % c) for c in range(N_CHUNKS)]
-        wr = [sb.tile([P, 2 * K], BF16, name="wr%d" % w) for w in range(2)]
+        wr = [sb.tile([P, 2 * K], BF16, name="wr%d" % mat) for mat in range(2)]
 
         def load_x(c):
             nc.sync.dma_start(out=xr[c][:], in_=x_rows[:, :, c * CHUNK : (c + 1) * CHUNK])
 
         load_x(0)
-        for w, weights in enumerate((W1, W2)):
+        for mat, weights in enumerate((W1, W2)):
             nc.sync.dma_start(
-                out=wr[w][:].rearrange("p (m k) -> p m k", m=2),
+                out=wr[mat][:].rearrange("p (m k) -> p m k", m=2),
                 in_=weights.rearrange("(m p) k -> p m k", p=P),
             )
         for c in range(1, N_CHUNKS):
@@ -56,9 +59,9 @@ def tile_selfspatialattentionmodule_pa_kernel(tc, x, W1, W2, out_0, out_1):
         xg = [sb.tile([P, CHUNK * PACK], BF16, name="xg%d" % c, align_bytes=ALIGN) for c in range(N_CHUNKS)]
         xq = [sb.tile([P, CHUNK], U32, name="xq%d" % c, align_bytes=ALIGN) for c in range(N_CHUNKS)]
         xs = [sb.tile([P, CHUNK], U8, name="xs%d" % c, align_bytes=ALIGN) for c in range(N_CHUNKS)]
-        wg = {wm: sb.tile([P, P * PACK], BF16, name="wg_%d_%d" % wm, align_bytes=ALIGN) for wm in weight_tiles}
-        wq = {wm: sb.tile([P, P], U32, name="wq_%d_%d" % wm, align_bytes=ALIGN) for wm in weight_tiles}
-        ws = {wm: sb.tile([P, P], U8, name="ws_%d_%d" % wm, align_bytes=ALIGN) for wm in weight_tiles}
+        wg = {key: sb.tile([P, P * PACK], BF16, name="wg_%d_%d" % key, align_bytes=ALIGN) for key in weight_tiles}
+        wq = {key: sb.tile([P, P], U32, name="wq_%d_%d" % key, align_bytes=ALIGN) for key in weight_tiles}
+        ws = {key: sb.tile([P, P], U8, name="ws_%d_%d" % key, align_bytes=ALIGN) for key in weight_tiles}
         top = [sb.tile([P, 2, PLANE], F32, name="top%d" % c) for c in range(N_CHUNKS)]
         c1p_sb = [sb.tile([P, 2, PLANE], F32, name="c1p_sb%d" % c) for c in range(N_CHUNKS)]
         c2_sb = {(c, m): sb.tile([P, CHUNK], F32, name="c2_sb_%d_%d" % (c, m)) for c in range(N_CHUNKS) for m in range(2)}
@@ -67,36 +70,46 @@ def tile_selfspatialattentionmodule_pa_kernel(tc, x, W1, W2, out_0, out_1):
         c2 = {}
         sums = {}
 
-        def transpose_w(w, m):
-            words = wr[w][:].bitcast(F32).rearrange("p (m q u) -> p m u q", m=2, u=2)
-            wt[w, m] = ps_c2.tile([P, 2, P], F32, name="wt_%d_%d" % (w, m), tag="c2")
+        def transpose_w(mat, m):
+            pairs = wr[mat][:].bitcast(F32).rearrange("p (m q u) -> p m u q", m=2, u=2)
+            wt[mat, m] = ps_c2.tile([P, 2, P], F32, name="wt_%d_%d" % (mat, m), tag="c2")
             for u in range(2):
-                nc.tensor.transpose(wt[w, m][:, u, :], words[:, m, u, :], identity[:])
+                nc.tensor.transpose(wt[mat, m][:, u, :], pairs[:, m, u, :], identity[:])
 
-        def copy_w(w, m):
+        def copy_w(mat, m):
             nc.scalar.copy(
-                out=wg[w, m][:].bitcast(F32).rearrange("p (o u) -> p o u", u=2),
-                in_=wt[w, m][:].rearrange("p u o -> p o u"),
+                out=wg[mat, m][:].bitcast(F32).rearrange("q (o u) -> q o u", u=2),
+                in_=wt[mat, m][:].rearrange("q u o -> q o u"),
             )
 
-        def quantise_w(w, m):
-            nc.vector.quantize_mx(out=wq[w, m][:].bitcast(FP8X4), scales=ws[w, m][:], in_=wg[w, m][:])
+        def quantise_w(mat, m):
+            nc.vector.quantize_mx(out=wq[mat, m][:].bitcast(FP8X4), scales=ws[mat, m][:], in_=wg[mat, m][:])
 
         def regroup(c):
-            words = xg[c][:].rearrange("p (a b i j t) -> p a b i j t", a=2, b=2, i=8, j=16, t=PACK)
-            rows = xr[c][:].rearrange("p t (i a j b) -> p a b i j t", i=8, a=2, j=16, b=2)
+            grouped = xg[c][:].rearrange(
+                "p (a b i g s t) -> p a b i g t s", a=2, b=2, i=WIN_ROWS, g=WIN_COLS // RUN, s=RUN, t=PACK
+            )
+            rows = xr[c][:].rearrange("p t (i a g s b) -> p a b i g t s", i=WIN_ROWS, a=2, g=WIN_COLS // RUN, s=RUN, b=2)
+            nc.vector.tensor_copy(out=grouped[:, 0, 0], in_=rows[:, 0, 0])
             for a in range(2):
-                nc.vector.tensor_copy(out=words[:, a, 0], in_=rows[:, a, 0])
-                nc.scalar.copy(out=words[:, a, 1], in_=rows[:, a, 1])
+                nc.scalar.copy(out=grouped[:, a, 1], in_=rows[:, a, 1])
+            nc.gpsimd.tensor_scalar(
+                out=xg[c][:].rearrange("p (a b i j t) -> p a b i j t", a=2, b=2, i=WIN_ROWS, j=WIN_COLS, t=PACK)[:, 1, 0],
+                in0=xr[c][:].rearrange("p t (i a j b) -> p a b i j t", i=WIN_ROWS, a=2, j=WIN_COLS, b=2)[:, 1, 0],
+                scalar1=1.0,
+                scalar2=0.0,
+                op0=ALU.mult,
+                op1=ALU.add,
+            )
 
         def quantise_x(c):
             nc.vector.quantize_mx(out=xq[c][:].bitcast(FP8X4), scales=xs[c][:], in_=xg[c][:])
 
-        def mx_pass(out, w, m, c, first, width, start, stop):
+        def mx_pass(out, mat, m, c, first, width, start, stop):
             nc.tensor.matmul_mx(
                 out=out,
-                lhsT=wq[w, m][:].bitcast(FP8X4),
-                lhsT_scale=ws[w, m][:],
+                lhsT=wq[mat, m][:].bitcast(FP8X4),
+                lhsT_scale=ws[mat, m][:],
                 rhs=xq[c][:, first : first + width].bitcast(FP8X4),
                 rhs_scale=xs[c][:, first : first + width],
                 start=start,
@@ -111,13 +124,13 @@ def tile_selfspatialattentionmodule_pa_kernel(tc, x, W1, W2, out_0, out_1):
                 mx_pass(c1[c, m][:], 0, m, c, 0, CHUNK, True, True)
                 mx_pass(c2[c, m][:], 1, m, c, 0, CHUNK, True, True)
             for m in range(2):
-                for place in range(4):
-                    mx_pass(sums[c][:, m, :], 0, m, c, place * PLANE, PLANE, place == 0, place == 3)
+                for plane in range(4):
+                    mx_pass(sums[c][:, m, :], 0, m, c, plane * PLANE, PLANE, plane == 0, plane == 3)
 
         def window_max(c, m):
             nc.vector.tensor_reduce(
                 out=top[c][:, m, :],
-                in_=c1[c, m][:].rearrange("p (place n) -> p n place", place=4),
+                in_=c1[c, m][:].rearrange("p (plane window) -> p window plane", plane=4),
                 axis=mybir.AxisListType.X,
                 op=ALU.max,
             )
@@ -132,19 +145,19 @@ def tile_selfspatialattentionmodule_pa_kernel(tc, x, W1, W2, out_0, out_1):
 
         def finish_c2(c, m):
             nc.scalar.copy(
-                out=c2_sb[c, m][:].rearrange("p (i a j b) -> p a i j b", i=8, a=2, j=16, b=2),
-                in_=c2[c, m][:].rearrange("p (a b i j) -> p a i j b", a=2, b=2, i=8, j=16),
+                out=c2_sb[c, m][:].rearrange("p (i a j b) -> p a i j b", i=WIN_ROWS, a=2, j=WIN_COLS, b=2),
+                in_=c2[c, m][:].rearrange("p (a b i j) -> p a i j b", a=2, b=2, i=WIN_ROWS, j=WIN_COLS),
             )
             nc.sync.dma_start(out=c2_out[:, m, c * CHUNK : (c + 1) * CHUNK], in_=c2_sb[c, m][:])
 
         regroup(0)
-        for w, m in weight_tiles:
-            transpose_w(w, m)
-        for w, m in weight_tiles:
-            copy_w(w, m)
+        for mat, m in weight_tiles:
+            transpose_w(mat, m)
+        for mat, m in weight_tiles:
+            copy_w(mat, m)
         quantise_x(0)
-        for w, m in weight_tiles:
-            quantise_w(w, m)
+        for mat, m in weight_tiles:
+            quantise_w(mat, m)
         products(0)
         for c in range(N_CHUNKS):
             if c + 1 < N_CHUNKS:

@@ -21,6 +21,8 @@ WIN_ROWS = 8
 WIN_COLS = 16
 PLANE = WIN_ROWS * WIN_COLS
 RUN = 4
+WHO = ("VSGS", "VSGS", "GSGS", "GSGS")
+WARM = 5
 ALIGN = 64
 
 
@@ -40,6 +42,10 @@ def tile_selfspatialattentionmodule_pa_kernel(tc, x, W1, W2, out_0, out_1):
 
         identity = sb.tile([P, P], F32, name="identity")
         masks.make_identity(nc, identity[:])
+
+        warm = ps_c1.tile([P, CHUNK], F32, name="warm", tag="c1")
+        for step in range(WARM):
+            nc.tensor.matmul(out=warm[:, :P], lhsT=identity[:], rhs=identity[:], start=True, stop=True)
 
         xr = [sb.tile([P, PACK, CHUNK], BF16, name="xr%d" % c) for c in range(N_CHUNKS)]
         wr = [sb.tile([P, 2 * K], BF16, name="wr%d" % mat) for mat in range(2)]
@@ -90,17 +96,22 @@ def tile_selfspatialattentionmodule_pa_kernel(tc, x, W1, W2, out_0, out_1):
                 "p (a b i g s t) -> p a b i g t s", a=2, b=2, i=WIN_ROWS, g=WIN_COLS // RUN, s=RUN, t=PACK
             )
             rows = xr[c][:].rearrange("p t (i a g s b) -> p a b i g t s", i=WIN_ROWS, a=2, g=WIN_COLS // RUN, s=RUN, b=2)
-            nc.vector.tensor_copy(out=grouped[:, 0, 0], in_=rows[:, 0, 0])
-            for a in range(2):
-                nc.scalar.copy(out=grouped[:, a, 1], in_=rows[:, a, 1])
-            nc.gpsimd.tensor_scalar(
-                out=xg[c][:].rearrange("p (a b i j t) -> p a b i j t", a=2, b=2, i=WIN_ROWS, j=WIN_COLS, t=PACK)[:, 1, 0],
-                in0=xr[c][:].rearrange("p t (i a j b) -> p a b i j t", i=WIN_ROWS, a=2, j=WIN_COLS, b=2)[:, 1, 0],
-                scalar1=1.0,
-                scalar2=0.0,
-                op0=ALU.mult,
-                op1=ALU.add,
-            )
+            for a, b in ((0, 0), (0, 1), (1, 1), (1, 0)):
+                engine = WHO[c][2 * a + b]
+                if engine == "V":
+                    nc.vector.tensor_copy(out=grouped[:, a, b], in_=rows[:, a, b])
+                elif engine == "S":
+                    nc.scalar.copy(out=grouped[:, a, b], in_=rows[:, a, b])
+            for a, b in ((1, 0), (0, 0), (1, 1)):
+                if WHO[c][2 * a + b] == "G":
+                    nc.gpsimd.tensor_scalar(
+                        out=xg[c][:].rearrange("p (a b i j t) -> p a b i j t", a=2, b=2, i=WIN_ROWS, j=WIN_COLS, t=PACK)[:, a, b],
+                        in0=xr[c][:].rearrange("p t (i a j b) -> p a b i j t", i=WIN_ROWS, a=2, j=WIN_COLS, b=2)[:, a, b],
+                        scalar1=1.0,
+                        scalar2=0.0,
+                        op0=ALU.mult,
+                        op1=ALU.add,
+                    )
 
         def quantise_x(c):
             nc.vector.quantize_mx(out=xq[c][:].bitcast(FP8X4), scales=xs[c][:], in_=xg[c][:])

@@ -55,10 +55,8 @@ def tile_selfspatialattentionmodule_pa_kernel(tc, x, W1, W2, out_0, out_1):
 
         load_x(0)
         for mat, weights in enumerate((W1, W2)):
-            nc.sync.dma_start(
-                out=wr[mat][:].rearrange("p (m k) -> p m k", m=2),
-                in_=weights.rearrange("(m p) k -> p m k", p=P),
-            )
+            for m in range(2):
+                nc.sync.dma_start(out=wr[mat][:, m * K : (m + 1) * K], in_=weights[m * P : (m + 1) * P, :])
         for c in range(1, N_CHUNKS):
             load_x(c)
 

@@ -179,6 +179,11 @@ def tile_selfspatialattentionmodule_pa_kernel(tc, x, W1, W2, out_0, out_1):
             finish_c2(c, 1)
             if c + 1 < N_CHUNKS:
                 products(c + 1)
-            add_mean(c, 0)
-            add_mean(c, 1)
-            store_c1p(c)
+            if c + 1 < N_CHUNKS:
+                add_mean(c, 0)
+                add_mean(c, 1)
+                store_c1p(c)
+            else:
+                for m in range(2):
+                    add_mean(c, m)
+                    nc.sync.dma_start(out=c1p_out[:, m, c * PLANE : (c + 1) * PLANE], in_=c1p_sb[c][:, m, :])

from contextlib import ExitStack

import concourse.masks as masks
import concourse.mybir as mybir

FLOPS = 2 * 512 * 512 * 2048

BF16 = mybir.dt.bfloat16
F32 = mybir.dt.float32
U32 = mybir.dt.uint32
U8 = mybir.dt.uint8
FP8X4 = mybir.dt.float8_e4m3fn_x4
ALU = mybir.AluOpType

P = 128
PACK = 4
K = P * PACK
CHUNK = 512
N_CHUNKS = 4
WIN_ROWS = 8
WIN_COLS = 16
PLANE = WIN_ROWS * WIN_COLS
RUN = 4
WHO = ("VSGS", "VSGS", "GSGS", "GSGS")
WARM = 5
ALIGN = 64


def tile_selfspatialattentionmodule_pa_kernel(tc, x, W1, W2, out_0, out_1):
    nc = tc.nc
    x_rows = x[0].rearrange("k h w -> k (h w)").rearrange("(p t) pixel -> p t pixel", t=PACK)
    c1p_out = out_0[0].rearrange("(m p) row col -> p m (row col)", p=P)
    c2_out = out_1[0].rearrange("(m p) h w -> p m (h w)", p=P)
    weight_tiles = [(mat, m) for mat in range(2) for m in range(2)]

    with ExitStack() as ctx:
        sb = ctx.enter_context(tc.tile_pool(name="sb", bufs=1))
        ps_c1 = ctx.enter_context(tc.psum_pool(name="ps_c1", bufs=3))
        ps_c2 = ctx.enter_context(tc.psum_pool(name="ps_c2", bufs=3))
        ps_sum = ctx.enter_context(tc.psum_pool(name="ps_sum", bufs=2))
        ctx.enter_context(tc.manual_schedule())

        identity = sb.tile([P, P], F32, name="identity")
        masks.make_identity(nc, identity[:])

        warm = ps_c1.tile([P, CHUNK], F32, name="warm", tag="c1")
        for step in range(WARM):
            nc.tensor.matmul(out=warm[:, :P], lhsT=identity[:], rhs=identity[:], start=True, stop=True)

        xr = [sb.tile([P, PACK, CHUNK], BF16, name="xr%d" % c) for c in range(N_CHUNKS)]
        wr = [sb.tile([P, 2 * K], BF16, name="wr%d" % mat) for mat in range(2)]

        def load_x(c):
            nc.sync.dma_start(out=xr[c][:], in_=x_rows[:, :, c * CHUNK : (c + 1) * CHUNK])

        load_x(0)
        for mat, weights in enumerate((W1, W2)):
            for m in range(2):
                nc.sync.dma_start(out=wr[mat][:, m * K : (m + 1) * K], in_=weights[m * P : (m + 1) * P, :])
        for c in range(1, N_CHUNKS):
            load_x(c)

        xg = [sb.tile([P, CHUNK * PACK], BF16, name="xg%d" % c, align_bytes=ALIGN) for c in range(N_CHUNKS)]
        xq = [sb.tile([P, CHUNK], U32, name="xq%d" % c, align_bytes=ALIGN) for c in range(N_CHUNKS)]
        xs = [sb.tile([P, CHUNK], U8, name="xs%d" % c, align_bytes=ALIGN) for c in range(N_CHUNKS)]
        wg = {key: sb.tile([P, P * PACK], BF16, name="wg_%d_%d" % key, align_bytes=ALIGN) for key in weight_tiles}
        wq = {key: sb.tile([P, P], U32, name="wq_%d_%d" % key, align_bytes=ALIGN) for key in weight_tiles}
        ws = {key: sb.tile([P, P], U8, name="ws_%d_%d" % key, align_bytes=ALIGN) for key in weight_tiles}
        top = [sb.tile([P, 2, PLANE], F32, name="top%d" % c) for c in range(N_CHUNKS)]
        c1p_sb = [sb.tile([P, 2, PLANE], F32, name="c1p_sb%d" % c) for c in range(N_CHUNKS)]
        c2_sb = {(c, m): sb.tile([P, CHUNK], F32, name="c2_sb_%d_%d" % (c, m)) for c in range(N_CHUNKS) for m in range(2)}
        wt = {}
        c1 = {}
        c2 = {}
        sums = {}

        def transpose_w(mat, m):
            pairs = wr[mat][:].bitcast(F32).rearrange("p (m q u) -> p m u q", m=2, u=2)
            wt[mat, m] = ps_c2.tile([P, 2, P], F32, name="wt_%d_%d" % (mat, m), tag="c2")
            for u in range(2):
                nc.tensor.transpose(wt[mat, m][:, u, :], pairs[:, m, u, :], identity[:])

        def copy_w(mat, m):
            nc.scalar.copy(
                out=wg[mat, m][:].bitcast(F32).rearrange("q (o u) -> q o u", u=2),
                in_=wt[mat, m][:].rearrange("q u o -> q o u"),
            )

        def quantise_w(mat, m):
            nc.vector.quantize_mx(out=wq[mat, m][:].bitcast(FP8X4), scales=ws[mat, m][:], in_=wg[mat, m][:])

        def regroup(c):
            grouped = xg[c][:].rearrange(
                "p (a b i g s t) -> p a b i g t s", a=2, b=2, i=WIN_ROWS, g=WIN_COLS // RUN, s=RUN, t=PACK
            )
            rows = xr[c][:].rearrange("p t (i a g s b) -> p a b i g t s", i=WIN_ROWS, a=2, g=WIN_COLS // RUN, s=RUN, b=2)
            for a, b in ((0, 0), (0, 1), (1, 1), (1, 0)):
                engine = WHO[c][2 * a + b]
                if engine == "V":
                    nc.vector.tensor_copy(out=grouped[:, a, b], in_=rows[:, a, b])
                elif engine == "S":
                    nc.scalar.copy(out=grouped[:, a, b], in_=rows[:, a, b])
            for a, b in ((1, 0), (0, 0), (1, 1)):
                if WHO[c][2 * a + b] == "G":
                    nc.gpsimd.tensor_scalar(
                        out=xg[c][:].rearrange("p (a b i j t) -> p a b i j t", a=2, b=2, i=WIN_ROWS, j=WIN_COLS, t=PACK)[:, a, b],
                        in0=xr[c][:].rearrange("p t (i a j b) -> p a b i j t", i=WIN_ROWS, a=2, j=WIN_COLS, b=2)[:, a, b],
                        scalar1=1.0,
                        scalar2=0.0,
                        op0=ALU.mult,
                        op1=ALU.add,
                    )

        def quantise_x(c):
            nc.vector.quantize_mx(out=xq[c][:].bitcast(FP8X4), scales=xs[c][:], in_=xg[c][:])

        def mx_pass(out, mat, m, c, first, width, start, stop):
            nc.tensor.matmul_mx(
                out=out,
                lhsT=wq[mat, m][:].bitcast(FP8X4),
                lhsT_scale=ws[mat, m][:],
                rhs=xq[c][:, first : first + width].bitcast(FP8X4),
                rhs_scale=xs[c][:, first : first + width],
                start=start,
                stop=stop,
            )

        def products(c):
            sums[c] = ps_sum.tile([P, 2, PLANE], F32, name="sums%d" % c, tag="sums")
            for m in range(2):
                c1[c, m] = ps_c1.tile([P, CHUNK], F32, name="c1_%d_%d" % (c, m), tag="c1")
                c2[c, m] = ps_c2.tile([P, CHUNK], F32, name="c2_%d_%d" % (c, m), tag="c2")
                mx_pass(c1[c, m][:], 0, m, c, 0, CHUNK, True, True)
                mx_pass(c2[c, m][:], 1, m, c, 0, CHUNK, True, True)
            for m in range(2):
                for plane in range(4):
                    mx_pass(sums[c][:, m, :], 0, m, c, plane * PLANE, PLANE, plane == 0, plane == 3)

        def window_max(c, m):
            nc.vector.tensor_reduce(
                out=top[c][:, m, :],
                in_=c1[c, m][:].rearrange("p (plane window) -> p window plane", plane=4),
                axis=mybir.AxisListType.X,
                op=ALU.max,
            )

        def add_mean(c, m):
            nc.vector.scalar_tensor_tensor(
                out=c1p_sb[c][:, m, :], in0=sums[c][:, m, :], scalar=0.25, in1=top[c][:, m, :], op0=ALU.mult, op1=ALU.add
            )

        def store_c1p(c):
            nc.sync.dma_start(out=c1p_out[:, :, c * PLANE : (c + 1) * PLANE], in_=c1p_sb[c][:])

        def finish_c2(c, m):
            nc.scalar.copy(
                out=c2_sb[c, m][:].rearrange("p (i a j b) -> p a i j b", i=WIN_ROWS, a=2, j=WIN_COLS, b=2),
                in_=c2[c, m][:].rearrange("p (a b i j) -> p a i j b", a=2, b=2, i=WIN_ROWS, j=WIN_COLS),
            )
            nc.sync.dma_start(out=c2_out[:, m, c * CHUNK : (c + 1) * CHUNK], in_=c2_sb[c, m][:])

        regroup(0)
        for mat, m in weight_tiles:
            transpose_w(mat, m)
        for mat, m in weight_tiles:
            copy_w(mat, m)
        quantise_x(0)
        for mat, m in weight_tiles:
            quantise_w(mat, m)
        products(0)
        for c in range(N_CHUNKS):
            if c + 1 < N_CHUNKS:
                regroup(c + 1)
            window_max(c, 0)
            if c + 1 < N_CHUNKS:
                quantise_x(c + 1)
            finish_c2(c, 0)
            window_max(c, 1)
            finish_c2(c, 1)
            if c + 1 < N_CHUNKS:
                products(c + 1)
            if c + 1 < N_CHUNKS:
                add_mean(c, 0)
                add_mean(c, 1)
                store_c1p(c)
            else:
                for m in range(2):
                    add_mean(c, m)
                    nc.sync.dma_start(out=c1p_out[:, m, c * PLANE : (c + 1) * PLANE], in_=c1p_sb[c][:, m, :])
